import numpy as np
import ml_dtypes


def mxq(x, axis, fmt="e4m3"):
    dtype, down = {"e4m3": (ml_dtypes.float8_e4m3fn, 7), "e5m2": (ml_dtypes.float8_e5m2, 14)}[fmt]
    v = np.moveaxis(np.asarray(x, np.float32).astype(ml_dtypes.bfloat16).astype(np.float64), axis, -1)
    blocks = v.reshape(v.shape[:-1] + (-1, 32))
    amax = np.abs(blocks).max(-1, keepdims=True)
    byte = np.maximum(np.where(amax > 0, np.frexp(amax)[1] - 1 + 127, 0) - down, 1)
    scale = np.exp2(byte - 127.0)
    codes = (blocks / scale).astype(np.float32).astype(dtype).astype(np.float64)
    return np.moveaxis((codes * scale).reshape(v.shape), -1, axis)


WIDE = False


def mx_kscale(k):
    if not WIDE:
        return np.ones(k)
    levels = np.array([10, -10, 5, -5, 0])
    a = np.random.permutation(np.resize(levels, k // 512 * 4)).reshape(k // 512, 4)
    idx = np.arange(k)
    return np.exp2(a[idx // 512, idx % 128 // 32])


BF16 = ml_dtypes.bfloat16


def bf(x):
    return np.asarray(x, np.float32).astype(BF16)


def f64(x):
    return np.asarray(x).astype(np.float64)


E2M1 = np.array([0.0, 0.5, 1.0, 1.5, 2.0, 3.0, 4.0, 6.0, -0.0, -0.5, -1.0, -1.5, -2.0, -3.0, -4.0, -6.0])


def pack_weight(w, fmt):
    k, n = w.shape
    w = f64(bf(w)).reshape(k // 32, 32, n)
    amax = np.abs(w).max(1)
    if fmt == "e4m3":
        byte = np.frexp(amax)[1] - 1 + 127 - 7
    else:
        mant, ex = np.frexp(amax / 6.0)
        byte = np.where(mant > 0.5, ex, ex - 1) + 127
    byte = np.clip(np.where(amax > 0, byte, 1), 1, 254)
    scaled = (w * np.exp2(127.0 - byte)[:, None, :]).reshape(k, n).astype(np.float32)
    by_word = np.ascontiguousarray(scaled.reshape(k // 512, 128, 4, n).transpose(0, 1, 3, 2))
    if fmt == "e4m3":
        words = by_word.astype(ml_dtypes.float8_e4m3fn).view(np.uint8)
    else:
        c = by_word.astype(ml_dtypes.float4_e2m1fn).view(np.uint8) & 0xF
        words = c[..., 0::2] | (c[..., 1::2] << 4)
    return np.ascontiguousarray(words), np.ascontiguousarray(byte.astype(np.uint8).reshape(k // 512, 16, n))


def unpack_weight(words, scales, fmt):
    g, p, n, _ = words.shape
    if fmt == "e4m3":
        vals = np.ascontiguousarray(words).view(ml_dtypes.float8_e4m3fn).astype(np.float64)
    else:
        nib = np.empty((g, p, n, 4), np.uint8)
        nib[..., 0::2] = words & 0xF
        nib[..., 1::2] = words >> 4
        vals = E2M1[nib]
    vals = vals * np.repeat(np.exp2(scales.astype(np.float64) - 127.0), 8, axis=1)[..., None]
    return vals.transpose(0, 1, 3, 2).reshape(g * 512, n)


B, S, D, F, P, NQ = 2, 128, 128, 4096, 512, 3
LN_EPS = 1e-5


def layernorm(v, g, b):
    m = v.mean(-1, keepdims=True)
    var = v.var(-1, keepdims=True)
    return (v - m) / np.sqrt(var + LN_EPS) * g + b


def setup_inputs():
    s = mx_kscale(P)
    in_proto = bf(np.random.standard_normal((NQ, F, P)) * s)
    pt_w = np.random.standard_normal((NQ, D, P)) / np.sqrt(P) / s
    cat = np.ascontiguousarray(pt_w.swapaxes(1, 2)).reshape(-1, D)
    words, scales = pack_weight(cat, "e4m3")
    return {"in_proto": in_proto,
            "pt_w_words": words,
            "pt_w_scales": scales,
            "pln_g": bf(1.0 + 0.1 * np.random.standard_normal((NQ, D))),
            "pln_b": bf(0.1 * np.random.standard_normal((NQ, D))),
            "proto_w": bf(np.random.standard_normal((NQ, F, D)) * 0.5)}


def reference(in_proto, pt_w_words, pt_w_scales, pln_g, pln_b, proto_w):
    prc = mxq(f64(in_proto), 2, "e4m3") @ unpack_weight(pt_w_words, pt_w_scales, "e4m3").reshape(NQ, P, D)
    return f64(proto_w) + layernorm(prc, f64(pln_g)[:, None, :], f64(pln_b)[:, None, :])

@@ -1,0 +1,246 @@
+from contextlib import ExitStack
+
+import concourse.mybir as mybir
+from concourse.masks import make_identity
+
+F32 = mybir.dt.float32
+BF16 = mybir.dt.bfloat16
+I32 = mybir.dt.int32
+U32 = mybir.dt.uint32
+U8 = mybir.dt.uint8
+FP8X4 = mybir.dt.float8_e4m3fn_x4
+ACT = mybir.ActivationFunctionType
+ALU = mybir.AluOpType
+
+P = 128
+NQ = 3
+F = 4096
+K = 512
+D = 128
+LN_EPS = 1e-5
+
+PACK = 4
+WORDS = K // 2
+TILES = F // P
+GROUP = 4
+GROUPS_PER_BANK = TILES // GROUP
+N_GROUPS = NQ * GROUPS_PER_BANK
+
+STATS_LAG = 2
+APPLY_LAG = 3
+
+FLOPS = 2 * NQ * F * K * D
+
+
+def tile_moietransformerblock_pb_t_e_kernel(
+    tc, in_proto, pt_w_words, pt_w_scales, pln_g, pln_b, proto_w, out
+):
+    nc = tc.nc
+
+    x_rows = in_proto.rearrange("n (p t) k -> n p t k", t=TILES)
+    pw_rows = proto_w.rearrange("n (p t) d -> n p t d", t=TILES)
+    out_rows = out.rearrange("n (p t) d -> n p t d", t=TILES)
+
+    def place(i):
+        n, g = divmod(i, GROUPS_PER_BANK)
+        return n, slice(g * GROUP, (g + 1) * GROUP)
+
+    with ExitStack() as ctx:
+        const = ctx.enter_context(tc.tile_pool(name="const", bufs=1))
+        x_pool = ctx.enter_context(tc.tile_pool(name="x", bufs=N_GROUPS))
+        pw_pool = ctx.enter_context(tc.tile_pool(name="pw", bufs=N_GROUPS))
+        res_pool = ctx.enter_context(tc.tile_pool(name="res", bufs=N_GROUPS))
+        quant = ctx.enter_context(tc.tile_pool(name="quant", bufs=3))
+        work = ctx.enter_context(tc.tile_pool(name="work", bufs=3))
+        stat = ctx.enter_context(tc.tile_pool(name="stat", bufs=6))
+        xt_pool = ctx.enter_context(tc.psum_pool(name="xt", bufs=4))
+        acc_pool = ctx.enter_context(tc.psum_pool(name="acc", bufs=4))
+        ctx.enter_context(tc.manual_schedule())
+
+        ident = const.tile([P, P], F32)
+        make_identity(nc, ident[:])
+        eps = const.tile([P, 1], F32)
+        nc.vector.memset(eps[:], LN_EPS)
+        w_scales = const.tile([P, NQ * D], U8, align_bytes=64)
+        w_scales_i32 = w_scales[:].bitcast(I32).rearrange("p (n c) -> p n c", n=NQ)
+        nc.vector.memset(w_scales[:].bitcast(I32), 0)
+
+        x_sb = {}
+        pw_sb = {}
+
+        def load_x(i):
+            n, tiles = place(i)
+            x_sb[i] = x_pool.tile([P, GROUP * K], BF16, name="x_sb")
+            nc.sync.dma_start(
+                out=x_sb[i][:].rearrange("p (a k) -> p a k", a=GROUP), in_=x_rows[n, :, tiles, :]
+            )
+
+        def load_pw(i):
+            n, tiles = place(i)
+            pw_sb[i] = pw_pool.tile([P, GROUP, D], BF16, name="pw_sb")
+            nc.sync.dma_start(out=pw_sb[i][:], in_=pw_rows[n, :, tiles, :])
+
+        load_x(0)
+        w_words = const.tile([P, NQ * D * PACK], U8, align_bytes=64)
+        nc.sync.dma_start(
+            out=w_words[:].bitcast(I32).rearrange("p (n c) -> p n c", n=NQ),
+            in_=pt_w_words.rearrange("n p d t -> n p (d t)").bitcast(I32).rearrange("n p c -> p n c"),
+        )
+        for quadrant in range(4):
+            nc.sync.dma_start(
+                out=w_scales_i32[32 * quadrant : 32 * quadrant + 4, :, :],
+                in_=pt_w_scales.bitcast(I32)[:, 4 * quadrant : 4 * quadrant + 4, :].rearrange(
+                    "n r c -> r n c"
+                ),
+            )
+        gain = const.tile([P, NQ * D], BF16)
+        nc.sync.dma_start(out=gain[:], in_=pln_g.rearrange("n d -> (n d)").partition_broadcast(P))
+        bias = const.tile([P, NQ * D], BF16)
+        nc.sync.dma_start(out=bias[:], in_=pln_b.rearrange("n d -> (n d)").partition_broadcast(P))
+        for i in range(N_GROUPS):
+            load_pw(i)
+            if i + 1 < N_GROUPS:
+                load_x(i + 1)
+
+        xt = {}
+        grouped = {}
+        codes = {}
+        scales = {}
+        acc = {}
+        neg_mean = {}
+        sum_sq = {}
+        std = {}
+        rstd = {}
+        result = {}
+
+        def transpose(i):
+            words = x_sb[i][:].bitcast(F32)
+            for half in range(GROUP // 2):
+                xt[i, half] = xt_pool.tile([P, 2, 2, P], F32, name="xt")
+                for a in range(2):
+                    first = (2 * half + a) * WORDS
+                    for u in range(2):
+                        nc.tensor.transpose(
+                            xt[i, half][:, a, u, :],
+                            words[:, first + u : first + WORDS : 2],
+                            ident[:],
+                        )
+
+        def copy_out(i, half):
+            if half == 0:
+                grouped[i] = quant.tile([P, GROUP * P * PACK], BF16, name="grouped", align_bytes=64)
+            dst = grouped[i][:].bitcast(F32).rearrange("p (a r u) -> p a r u", a=GROUP, u=2)
+            nc.scalar.copy(
+                out=dst[:, 2 * half : 2 * half + 2, :, :],
+                in_=xt[i, half][:].rearrange("p a u r -> p a r u"),
+            )
+
+        def quantise(i):
+            codes[i] = quant.tile([P, GROUP * P], U32, name="codes", align_bytes=64)
+            scales[i] = quant.tile([P, GROUP * P], U8, name="scales", align_bytes=64)
+            nc.vector.quantize_mx(
+                out=codes[i][:].bitcast(FP8X4), scales=scales[i][:], in_=grouped[i][:]
+            )
+
+        def multiply(i):
+            n, tiles = place(i)
+            acc[i] = acc_pool.tile([P, GROUP, D], F32, name="acc")
+            for a in range(GROUP):
+                rows = slice(a * P, (a + 1) * P)
+                nc.tensor.matmul_mx(
+                    out=acc[i][:, a, :],
+                    lhsT=codes[i][:, rows].bitcast(FP8X4),
+                    lhsT_scale=scales[i][:, rows],
+                    rhs=w_words[:, n * D * PACK : (n + 1) * D * PACK].bitcast(FP8X4),
+                    rhs_scale=w_scales[:, n * D : (n + 1) * D],
+                    start=True,
+                    stop=True,
+                )
+
+        def take_mean(i):
+            neg_mean[i] = stat.tile([P, GROUP], F32, name="neg_mean")
+            unused = work.tile([P, GROUP, D], BF16, name="unused_mean")
+            for a in range(GROUP):
+                nc.scalar.activation(
+                    out=unused[:, a, :],
+                    in_=acc[i][:, a, :],
+                    func=ACT.Identity,
+                    scale=-1.0 / D,
+                    accum_out=neg_mean[i][:, a : a + 1],
+                )
+
+        def take_variance(i):
+            sum_sq[i] = stat.tile([P, GROUP], F32, name="sum_sq")
+            unused = work.tile([P, GROUP, D], BF16, name="unused_sq")
+            for a in range(GROUP):
+                nc.scalar.activation(
+                    out=unused[:, a, :],
+                    in_=acc[i][:, a, :],
+                    func=ACT.Square,
+                    bias=neg_mean[i][:, a : a + 1],
+                    accum_out=sum_sq[i][:, a : a + 1],
+                )
+
+        def take_std(i):
+            std[i] = stat.tile([P, GROUP], F32, name="std")
+            nc.scalar.activation(
+                out=std[i][:], in_=sum_sq[i][:], func=ACT.Sqrt, scale=1.0 / D, bias=eps[:]
+            )
+
+        def add_bias(i):
+            n, tiles = place(i)
+            result[i] = res_pool.tile([P, GROUP, D], F32, name="result")
+            nc.vector.tensor_tensor(
+                out=result[i][:],
+                in0=pw_sb[i][:],
+                in1=bias[:, n * D : (n + 1) * D].unsqueeze(1).to_broadcast([P, GROUP, D]),
+                op=ALU.add,
+            )
+
+        def normalise(i):
+            n, tiles = place(i)
+            rstd[i] = stat.tile([P, GROUP], F32, name="rstd")
+            nc.vector.reciprocal(out=rstd[i][:], in_=std[i][:])
+            centred = work.tile([P, GROUP, D], F32, name="centred")
+            for a in range(GROUP):
+                nc.vector.scalar_tensor_tensor(
+                    out=centred[:, a, :],
+                    in0=acc[i][:, a, :],
+                    scalar=neg_mean[i][:, a : a + 1],
+                    in1=gain[:, n * D : (n + 1) * D],
+                    op0=ALU.add,
+                    op1=ALU.mult,
+                )
+            for a in range(GROUP):
+                nc.vector.scalar_tensor_tensor(
+                    out=result[i][:, a, :],
+                    in0=centred[:, a, :],
+                    scalar=rstd[i][:, a : a + 1],
+                    in1=result[i][:, a, :],
+                    op0=ALU.mult,
+                    op1=ALU.add,
+                )
+            nc.sync.dma_start(out=out_rows[n, :, tiles, :], in_=result[i][:])
+
+        transpose(0)
+        for i in range(N_GROUPS + APPLY_LAG):
+            if 0 <= i - STATS_LAG < N_GROUPS:
+                take_mean(i - STATS_LAG)
+            if i < N_GROUPS:
+                copy_out(i, 0)
+            if 0 <= i - STATS_LAG < N_GROUPS:
+                take_variance(i - STATS_LAG)
+            if i < N_GROUPS:
+                copy_out(i, 1)
+            if 0 <= i - STATS_LAG < N_GROUPS:
+                take_std(i - STATS_LAG)
+            if i < N_GROUPS:
+                add_bias(i)
+            if i - APPLY_LAG >= 0:
+                normalise(i - APPLY_LAG)
+            if i < N_GROUPS:
+                quantise(i)
+            if i + 1 < N_GROUPS:
+                transpose(i + 1)
+            if i < N_GROUPS:
+                multiply(i)

@@ -28,6 +28,8 @@ N_GROUPS = NQ * GROUPS_PER_BANK
 
 STATS_LAG = 2
 APPLY_LAG = 3
+BIAS_LAG = 1
+VECTOR_COPY_EVERY = 3
 
 FLOPS = 2 * NQ * F * K * D
 
@@ -61,6 +63,8 @@ def tile_moietransformerblock_pb_t_e_kernel(
         make_identity(nc, ident[:])
         eps = const.tile([P, 1], F32)
         nc.vector.memset(eps[:], LN_EPS)
+        table_warmer = const.tile([P, 1], F32)
+        nc.scalar.sqrt(out=table_warmer[:], in_=eps[:])
         w_scales = const.tile([P, NQ * D], U8, align_bytes=64)
         w_scales_i32 = w_scales[:].bitcast(I32).rearrange("p (n c) -> p n c", n=NQ)
         nc.vector.memset(w_scales[:].bitcast(I32), 0)
@@ -93,14 +97,15 @@ def tile_moietransformerblock_pb_t_e_kernel(
                     "n r c -> r n c"
                 ),
             )
+        load_x(1)
         gain = const.tile([P, NQ * D], BF16)
         nc.sync.dma_start(out=gain[:], in_=pln_g.rearrange("n d -> (n d)").partition_broadcast(P))
         bias = const.tile([P, NQ * D], BF16)
         nc.sync.dma_start(out=bias[:], in_=pln_b.rearrange("n d -> (n d)").partition_broadcast(P))
         for i in range(N_GROUPS):
             load_pw(i)
-            if i + 1 < N_GROUPS:
-                load_x(i + 1)
+            if i + 2 < N_GROUPS:
+                load_x(i + 2)
 
         xt = {}
         grouped = {}
@@ -130,10 +135,12 @@ def tile_moietransformerblock_pb_t_e_kernel(
             if half == 0:
                 grouped[i] = quant.tile([P, GROUP * P * PACK], BF16, name="grouped", align_bytes=64)
             dst = grouped[i][:].bitcast(F32).rearrange("p (a r u) -> p a r u", a=GROUP, u=2)
-            nc.scalar.copy(
-                out=dst[:, 2 * half : 2 * half + 2, :, :],
-                in_=xt[i, half][:].rearrange("p a u r -> p a r u"),
-            )
+            dst = dst[:, 2 * half : 2 * half + 2, :, :]
+            src = xt[i, half][:].rearrange("p a u r -> p a r u")
+            if half == 0 and i % VECTOR_COPY_EVERY == 0:
+                nc.vector.tensor_copy(out=dst, in_=src)
+            else:
+                nc.scalar.copy(out=dst, in_=src)
 
         def quantise(i):
             codes[i] = quant.tile([P, GROUP * P], U32, name="codes", align_bytes=64)
@@ -234,10 +241,10 @@ def tile_moietransformerblock_pb_t_e_kernel(
                 copy_out(i, 1)
             if 0 <= i - STATS_LAG < N_GROUPS:
                 take_std(i - STATS_LAG)
-            if i < N_GROUPS:
-                add_bias(i)
             if i - APPLY_LAG >= 0:
                 normalise(i - APPLY_LAG)
+            if 0 <= i - BIAS_LAG < N_GROUPS:
+                add_bias(i - BIAS_LAG)
             if i < N_GROUPS:
                 quantise(i)
             if i + 1 < N_GROUPS:

@@ -26,10 +26,7 @@ GROUP = 4
 GROUPS_PER_BANK = TILES // GROUP
 N_GROUPS = NQ * GROUPS_PER_BANK
 
-STATS_LAG = 2
-APPLY_LAG = 3
-BIAS_LAG = 1
-VECTOR_COPY_EVERY = 3
+VECTOR_COPY_EVERY = 5
 
 FLOPS = 2 * NQ * F * K * D
 
@@ -59,15 +56,24 @@ def tile_moietransformerblock_pb_t_e_kernel(
         acc_pool = ctx.enter_context(tc.psum_pool(name="acc", bufs=4))
         ctx.enter_context(tc.manual_schedule())
 
+        vectors = const.tile([P, 2, GROUP * D], BF16)
+        nc.vector.memset(vectors[:], 0.0)
+        for v, vector in enumerate((pln_g, pln_b)):
+            nc.scalar.dma_start(
+                out=vectors[0:1, v, 0 : NQ * D], in_=vector.rearrange("n d -> (n d)").unsqueeze(0)
+            )
+        ones = const.tile([P, P], BF16)
+        nc.vector.memset(ones[:], 1.0)
         ident = const.tile([P, P], F32)
         make_identity(nc, ident[:])
         eps = const.tile([P, 1], F32)
         nc.vector.memset(eps[:], LN_EPS)
-        table_warmer = const.tile([P, 1], F32)
-        nc.scalar.sqrt(out=table_warmer[:], in_=eps[:])
         w_scales = const.tile([P, NQ * D], U8, align_bytes=64)
         w_scales_i32 = w_scales[:].bitcast(I32).rearrange("p (n c) -> p n c", n=NQ)
         nc.vector.memset(w_scales[:].bitcast(I32), 0)
+
+        table_warmer = const.tile([P, 1], F32)
+        nc.scalar.activation(out=table_warmer[:], in_=eps[:], func=ACT.Abs_reciprocal_sqrt)
 
         x_sb = {}
         pw_sb = {}
@@ -85,6 +91,7 @@ def tile_moietransformerblock_pb_t_e_kernel(
             nc.sync.dma_start(out=pw_sb[i][:], in_=pw_rows[n, :, tiles, :])
 
         load_x(0)
+        load_x(1)
         w_words = const.tile([P, NQ * D * PACK], U8, align_bytes=64)
         nc.sync.dma_start(
             out=w_words[:].bitcast(I32).rearrange("p (n c) -> p n c", n=NQ),
@@ -97,15 +104,18 @@ def tile_moietransformerblock_pb_t_e_kernel(
                     "n r c -> r n c"
                 ),
             )
-        load_x(1)
-        gain = const.tile([P, NQ * D], BF16)
-        nc.sync.dma_start(out=gain[:], in_=pln_g.rearrange("n d -> (n d)").partition_broadcast(P))
-        bias = const.tile([P, NQ * D], BF16)
-        nc.sync.dma_start(out=bias[:], in_=pln_b.rearrange("n d -> (n d)").partition_broadcast(P))
+        load_x(2)
         for i in range(N_GROUPS):
             load_pw(i)
-            if i + 2 < N_GROUPS:
-                load_x(i + 2)
+            if i + 3 < N_GROUPS:
+                load_x(i + 3)
+
+        gain = const.tile([P, NQ * D], F32)
+        bias = const.tile([P, NQ * D], F32)
+        for v, spread in enumerate((gain, bias)):
+            repeated = acc_pool.tile([P, GROUP * D], F32, name="acc")
+            nc.tensor.matmul(out=repeated[:], lhsT=ones[:], rhs=vectors[:, v, :], start=True, stop=True)
+            nc.vector.tensor_copy(out=spread[:], in_=repeated[:, 0 : NQ * D])
 
         xt = {}
         grouped = {}
@@ -114,8 +124,9 @@ def tile_moietransformerblock_pb_t_e_kernel(
         acc = {}
         neg_mean = {}
         sum_sq = {}
-        std = {}
+        scaled_x = {}
         rstd = {}
+        centred = {}
         result = {}
 
         def transpose(i):
@@ -166,32 +177,37 @@ def tile_moietransformerblock_pb_t_e_kernel(
 
         def take_mean(i):
             neg_mean[i] = stat.tile([P, GROUP], F32, name="neg_mean")
-            unused = work.tile([P, GROUP, D], BF16, name="unused_mean")
+            scaled_x[i] = work.tile([P, GROUP, D], F32, name="scaled_x")
             for a in range(GROUP):
                 nc.scalar.activation(
-                    out=unused[:, a, :],
+                    out=scaled_x[i][:, a, :],
                     in_=acc[i][:, a, :],
-                    func=ACT.Identity,
+                    func=ACT.Copy,
                     scale=-1.0 / D,
                     accum_out=neg_mean[i][:, a : a + 1],
                 )
 
         def take_variance(i):
             sum_sq[i] = stat.tile([P, GROUP], F32, name="sum_sq")
-            unused = work.tile([P, GROUP, D], BF16, name="unused_sq")
+            unused = work.tile([P, GROUP, D], BF16, name="unused")
             for a in range(GROUP):
                 nc.scalar.activation(
                     out=unused[:, a, :],
-                    in_=acc[i][:, a, :],
+                    in_=scaled_x[i][:, a, :],
                     func=ACT.Square,
+                    scale=-1.0 * D,
                     bias=neg_mean[i][:, a : a + 1],
                     accum_out=sum_sq[i][:, a : a + 1],
                 )
 
-        def take_std(i):
-            std[i] = stat.tile([P, GROUP], F32, name="std")
+        def take_rstd(i):
+            rstd[i] = stat.tile([P, GROUP], F32, name="rstd")
             nc.scalar.activation(
-                out=std[i][:], in_=sum_sq[i][:], func=ACT.Sqrt, scale=1.0 / D, bias=eps[:]
+                out=rstd[i][:],
+                in_=sum_sq[i][:],
+                func=ACT.Abs_reciprocal_sqrt,
+                scale=1.0 / D,
+                bias=eps[:],
             )
 
         def add_bias(i):
@@ -204,24 +220,25 @@ def tile_moietransformerblock_pb_t_e_kernel(
                 op=ALU.add,
             )
 
-        def normalise(i):
+        def centre(i):
             n, tiles = place(i)
-            rstd[i] = stat.tile([P, GROUP], F32, name="rstd")
-            nc.vector.reciprocal(out=rstd[i][:], in_=std[i][:])
-            centred = work.tile([P, GROUP, D], F32, name="centred")
+            centred[i] = work.tile([P, GROUP, D], F32, name="centred")
             for a in range(GROUP):
                 nc.vector.scalar_tensor_tensor(
-                    out=centred[:, a, :],
+                    out=centred[i][:, a, :],
                     in0=acc[i][:, a, :],
                     scalar=neg_mean[i][:, a : a + 1],
                     in1=gain[:, n * D : (n + 1) * D],
                     op0=ALU.add,
                     op1=ALU.mult,
                 )
+
+        def finish(i):
+            n, tiles = place(i)
             for a in range(GROUP):
                 nc.vector.scalar_tensor_tensor(
                     out=result[i][:, a, :],
-                    in0=centred[:, a, :],
+                    in0=centred[i][:, a, :],
                     scalar=rstd[i][:, a : a + 1],
                     in1=result[i][:, a, :],
                     op0=ALU.mult,
@@ -229,25 +246,29 @@ def tile_moietransformerblock_pb_t_e_kernel(
                 )
             nc.sync.dma_start(out=out_rows[n, :, tiles, :], in_=result[i][:])
 
+        def in_range(i):
+            return 0 <= i < N_GROUPS
+
         transpose(0)
-        for i in range(N_GROUPS + APPLY_LAG):
-            if 0 <= i - STATS_LAG < N_GROUPS:
-                take_mean(i - STATS_LAG)
-            if i < N_GROUPS:
-                copy_out(i, 0)
-            if 0 <= i - STATS_LAG < N_GROUPS:
-                take_variance(i - STATS_LAG)
-            if i < N_GROUPS:
-                copy_out(i, 1)
-            if 0 <= i - STATS_LAG < N_GROUPS:
-                take_std(i - STATS_LAG)
-            if i - APPLY_LAG >= 0:
-                normalise(i - APPLY_LAG)
-            if 0 <= i - BIAS_LAG < N_GROUPS:
-                add_bias(i - BIAS_LAG)
-            if i < N_GROUPS:
-                quantise(i)
-            if i + 1 < N_GROUPS:
+        for i in range(N_GROUPS + 3):
+            if in_range(i - 1):
+                quantise(i - 1)
+                multiply(i - 1)
+            if in_range(i + 1):
                 transpose(i + 1)
-            if i < N_GROUPS:
-                multiply(i)
+            if in_range(i - 2):
+                take_mean(i - 2)
+            if in_range(i):
+                copy_out(i, 0)
+            if in_range(i - 2):
+                take_variance(i - 2)
+            if in_range(i):
+                copy_out(i, 1)
+            if in_range(i - 2):
+                take_rstd(i - 2)
+            if in_range(i - 3):
+                finish(i - 3)
+            if in_range(i - 1):
+                add_bias(i - 1)
+            if in_range(i - 2):
+                centre(i - 2)

@@ -26,8 +26,6 @@ GROUP = 4
 GROUPS_PER_BANK = TILES // GROUP
 N_GROUPS = NQ * GROUPS_PER_BANK
 
-VECTOR_COPY_EVERY = 5
-
 FLOPS = 2 * NQ * F * K * D
 
 
@@ -56,12 +54,10 @@ def tile_moietransformerblock_pb_t_e_kernel(
         acc_pool = ctx.enter_context(tc.psum_pool(name="acc", bufs=4))
         ctx.enter_context(tc.manual_schedule())
 
-        vectors = const.tile([P, 2, GROUP * D], BF16)
+        vectors = const.tile([P, NQ, 2, D], BF16)
         nc.vector.memset(vectors[:], 0.0)
         for v, vector in enumerate((pln_g, pln_b)):
-            nc.scalar.dma_start(
-                out=vectors[0:1, v, 0 : NQ * D], in_=vector.rearrange("n d -> (n d)").unsqueeze(0)
-            )
+            nc.scalar.dma_start(out=vectors[0:1, :, v, :], in_=vector.unsqueeze(0))
         ones = const.tile([P, P], BF16)
         nc.vector.memset(ones[:], 1.0)
         ident = const.tile([P, P], F32)
@@ -110,13 +106,6 @@ def tile_moietransformerblock_pb_t_e_kernel(
             if i + 3 < N_GROUPS:
                 load_x(i + 3)
 
-        gain = const.tile([P, NQ * D], F32)
-        bias = const.tile([P, NQ * D], F32)
-        for v, spread in enumerate((gain, bias)):
-            repeated = acc_pool.tile([P, GROUP * D], F32, name="acc")
-            nc.tensor.matmul(out=repeated[:], lhsT=ones[:], rhs=vectors[:, v, :], start=True, stop=True)
-            nc.vector.tensor_copy(out=spread[:], in_=repeated[:, 0 : NQ * D])
-
         xt = {}
         grouped = {}
         codes = {}
@@ -128,6 +117,18 @@ def tile_moietransformerblock_pb_t_e_kernel(
         rstd = {}
         centred = {}
         result = {}
+        gain_bias = const.tile([P, NQ, 2, D], F32)
+
+        def spread(n):
+            repeated = acc_pool.tile([P, 2, D], F32, name="acc")
+            nc.tensor.matmul(
+                out=repeated[:].rearrange("p v d -> p (v d)"),
+                lhsT=ones[:],
+                rhs=vectors[:, n, :, :].rearrange("p v d -> p (v d)"),
+                start=True,
+                stop=True,
+            )
+            nc.vector.tensor_copy(out=gain_bias[:, n, :, :], in_=repeated[:])
 
         def transpose(i):
             words = x_sb[i][:].bitcast(F32)
@@ -146,12 +147,10 @@ def tile_moietransformerblock_pb_t_e_kernel(
             if half == 0:
                 grouped[i] = quant.tile([P, GROUP * P * PACK], BF16, name="grouped", align_bytes=64)
             dst = grouped[i][:].bitcast(F32).rearrange("p (a r u) -> p a r u", a=GROUP, u=2)
-            dst = dst[:, 2 * half : 2 * half + 2, :, :]
-            src = xt[i, half][:].rearrange("p a u r -> p a r u")
-            if half == 0 and i % VECTOR_COPY_EVERY == 0:
-                nc.vector.tensor_copy(out=dst, in_=src)
-            else:
-                nc.scalar.copy(out=dst, in_=src)
+            nc.scalar.copy(
+                out=dst[:, 2 * half : 2 * half + 2, :, :],
+                in_=xt[i, half][:].rearrange("p a u r -> p a r u"),
+            )
 
         def quantise(i):
             codes[i] = quant.tile([P, GROUP * P], U32, name="codes", align_bytes=64)
@@ -216,7 +215,7 @@ def tile_moietransformerblock_pb_t_e_kernel(
             nc.vector.tensor_tensor(
                 out=result[i][:],
                 in0=pw_sb[i][:],
-                in1=bias[:, n * D : (n + 1) * D].unsqueeze(1).to_broadcast([P, GROUP, D]),
+                in1=gain_bias[:, n, 1, :].unsqueeze(1).to_broadcast([P, GROUP, D]),
                 op=ALU.add,
             )
 
@@ -228,7 +227,7 @@ def tile_moietransformerblock_pb_t_e_kernel(
                     out=centred[i][:, a, :],
                     in0=acc[i][:, a, :],
                     scalar=neg_mean[i][:, a : a + 1],
-                    in1=gain[:, n * D : (n + 1) * D],
+                    in1=gain_bias[:, n, 0, :],
                     op0=ALU.add,
                     op1=ALU.mult,
                 )
@@ -252,6 +251,8 @@ def tile_moietransformerblock_pb_t_e_kernel(
         transpose(0)
         for i in range(N_GROUPS + 3):
             if in_range(i - 1):
+                if (i - 1) % GROUPS_PER_BANK == 0:
+                    spread((i - 1) // GROUPS_PER_BANK)
                 quantise(i - 1)
                 multiply(i - 1)
             if in_range(i + 1):
@@ -266,9 +267,8 @@ def tile_moietransformerblock_pb_t_e_kernel(
                 copy_out(i, 1)
             if in_range(i - 2):
                 take_rstd(i - 2)
-            if in_range(i - 3):
-                finish(i - 3)
+                centre(i - 2)
             if in_range(i - 1):
                 add_bias(i - 1)
-            if in_range(i - 2):
-                centre(i - 2)
+            if in_range(i - 3):
+                finish(i - 3)

@@ -111,8 +111,8 @@ def tile_moietransformerblock_pb_t_e_kernel(
         codes = {}
         scales = {}
         acc = {}
-        neg_mean = {}
-        sum_sq = {}
+        mean_var = {}
+        halves = {}
         scaled_x = {}
         rstd = {}
         centred = {}
@@ -174,40 +174,54 @@ def tile_moietransformerblock_pb_t_e_kernel(
                     stop=True,
                 )
 
+        def scalar_tiles(i):
+            return GROUP - 1 if i % 2 == 0 else GROUP
+
         def take_mean(i):
-            neg_mean[i] = stat.tile([P, GROUP], F32, name="neg_mean")
+            mean_var[i] = stat.tile([P, GROUP, 2], F32, name="mean_var")
             scaled_x[i] = work.tile([P, GROUP, D], F32, name="scaled_x")
-            for a in range(GROUP):
+            for a in range(scalar_tiles(i)):
                 nc.scalar.activation(
                     out=scaled_x[i][:, a, :],
                     in_=acc[i][:, a, :],
                     func=ACT.Copy,
-                    scale=-1.0 / D,
-                    accum_out=neg_mean[i][:, a : a + 1],
+                    scale=1.0 / D,
+                    accum_out=mean_var[i][:, a, 0:1],
                 )
 
+        def vector_stats(i):
+            for a in range(scalar_tiles(i), GROUP):
+                halves[i, a] = stat.tile([P, 6], F32, name="halves")
+                nc.vector.bn_stats(out=halves[i, a][:], in_=acc[i][:, a, :])
+
+        def vector_aggregate(i):
+            for a in range(scalar_tiles(i), GROUP):
+                nc.vector.bn_aggr(out=mean_var[i][:, a, :], in_=halves[i, a][:])
+
         def take_variance(i):
-            sum_sq[i] = stat.tile([P, GROUP], F32, name="sum_sq")
             unused = work.tile([P, GROUP, D], BF16, name="unused")
-            for a in range(GROUP):
+            for a in range(scalar_tiles(i)):
                 nc.scalar.activation(
                     out=unused[:, a, :],
                     in_=scaled_x[i][:, a, :],
                     func=ACT.Square,
                     scale=-1.0 * D,
-                    bias=neg_mean[i][:, a : a + 1],
-                    accum_out=sum_sq[i][:, a : a + 1],
+                    bias=mean_var[i][:, a, 0:1],
+                    accum_out=mean_var[i][:, a, 1:2],
                 )
 
         def take_rstd(i):
             rstd[i] = stat.tile([P, GROUP], F32, name="rstd")
-            nc.scalar.activation(
-                out=rstd[i][:],
-                in_=sum_sq[i][:],
-                func=ACT.Abs_reciprocal_sqrt,
-                scale=1.0 / D,
-                bias=eps[:],
-            )
+            own = scalar_tiles(i)
+            for first, last, scale in ((0, own, 1.0 / D), (own, GROUP, 1.0)):
+                if first < last:
+                    nc.scalar.activation(
+                        out=rstd[i][:, first:last],
+                        in_=mean_var[i][:, first:last, 1],
+                        func=ACT.Abs_reciprocal_sqrt,
+                        scale=scale,
+                        bias=eps[:],
+                    )
 
         def add_bias(i):
             n, tiles = place(i)
@@ -219,16 +233,17 @@ def tile_moietransformerblock_pb_t_e_kernel(
                 op=ALU.add,
             )
 
-        def centre(i):
+        def centre(i, first, last):
             n, tiles = place(i)
-            centred[i] = work.tile([P, GROUP, D], F32, name="centred")
-            for a in range(GROUP):
+            if first == 0:
+                centred[i] = work.tile([P, GROUP, D], F32, name="centred")
+            for a in range(first, last):
                 nc.vector.scalar_tensor_tensor(
                     out=centred[i][:, a, :],
                     in0=acc[i][:, a, :],
-                    scalar=neg_mean[i][:, a : a + 1],
+                    scalar=mean_var[i][:, a, 0:1],
                     in1=gain_bias[:, n, 0, :],
-                    op0=ALU.add,
+                    op0=ALU.subtract,
                     op1=ALU.mult,
                 )
 
@@ -266,9 +281,14 @@ def tile_moietransformerblock_pb_t_e_kernel(
             if in_range(i):
                 copy_out(i, 1)
             if in_range(i - 2):
+                vector_stats(i - 2)
+                centre(i - 2, 0, 2)
+                vector_aggregate(i - 2)
                 take_rstd(i - 2)
-                centre(i - 2)
+                centre(i - 2, 2, 3)
             if in_range(i - 1):
                 add_bias(i - 1)
+            if in_range(i - 2):
+                centre(i - 2, 3, GROUP)
             if in_range(i - 3):
                 finish(i - 3)

@@ -25,6 +25,8 @@ TILES = F // P
 GROUP = 4
 GROUPS_PER_BANK = TILES // GROUP
 N_GROUPS = NQ * GROUPS_PER_BANK
+POOL_TILES = 3
+SHIFTED_BUFS = 4
 
 FLOPS = 2 * NQ * F * K * D
 
@@ -50,10 +52,15 @@ def tile_moietransformerblock_pb_t_e_kernel(
         quant = ctx.enter_context(tc.tile_pool(name="quant", bufs=3))
         work = ctx.enter_context(tc.tile_pool(name="work", bufs=3))
         stat = ctx.enter_context(tc.tile_pool(name="stat", bufs=6))
+        shift_pool = ctx.enter_context(tc.tile_pool(name="shift", bufs=SHIFTED_BUFS))
         xt_pool = ctx.enter_context(tc.psum_pool(name="xt", bufs=4))
         acc_pool = ctx.enter_context(tc.psum_pool(name="acc", bufs=4))
         ctx.enter_context(tc.manual_schedule())
 
+        eps = const.tile([P, 1], F32)
+        nc.vector.memset(eps[:], LN_EPS)
+        table_warmer = const.tile([P, 1], F32)
+        nc.scalar.activation(out=table_warmer[:], in_=eps[:], func=ACT.Abs_reciprocal_sqrt)
         vectors = const.tile([P, NQ, 2, D], BF16)
         nc.vector.memset(vectors[:], 0.0)
         for v, vector in enumerate((pln_g, pln_b)):
@@ -62,32 +69,32 @@ def tile_moietransformerblock_pb_t_e_kernel(
         nc.vector.memset(ones[:], 1.0)
         ident = const.tile([P, P], F32)
         make_identity(nc, ident[:])
-        eps = const.tile([P, 1], F32)
-        nc.vector.memset(eps[:], LN_EPS)
         w_scales = const.tile([P, NQ * D], U8, align_bytes=64)
         w_scales_i32 = w_scales[:].bitcast(I32).rearrange("p (n c) -> p n c", n=NQ)
         nc.vector.memset(w_scales[:].bitcast(I32), 0)
 
-        table_warmer = const.tile([P, 1], F32)
-        nc.scalar.activation(out=table_warmer[:], in_=eps[:], func=ACT.Abs_reciprocal_sqrt)
-
         x_sb = {}
         pw_sb = {}
 
-        def load_x(i):
+        def load_x(i, pieces):
             n, tiles = place(i)
             x_sb[i] = x_pool.tile([P, GROUP * K], BF16, name="x_sb")
-            nc.sync.dma_start(
-                out=x_sb[i][:].rearrange("p (a k) -> p a k", a=GROUP), in_=x_rows[n, :, tiles, :]
-            )
+            step = GROUP // pieces
+            for first in range(0, GROUP, step):
+                nc.sync.dma_start(
+                    out=x_sb[i][:, first * K : (first + step) * K].rearrange(
+                        "p (a k) -> p a k", a=step
+                    ),
+                    in_=x_rows[n, :, tiles.start + first : tiles.start + first + step, :],
+                )
 
         def load_pw(i):
             n, tiles = place(i)
             pw_sb[i] = pw_pool.tile([P, GROUP, D], BF16, name="pw_sb")
             nc.sync.dma_start(out=pw_sb[i][:], in_=pw_rows[n, :, tiles, :])
 
-        load_x(0)
-        load_x(1)
+        load_x(0, 2)
+        load_x(1, 1)
         w_words = const.tile([P, NQ * D * PACK], U8, align_bytes=64)
         nc.sync.dma_start(
             out=w_words[:].bitcast(I32).rearrange("p (n c) -> p n c", n=NQ),
@@ -100,11 +107,12 @@ def tile_moietransformerblock_pb_t_e_kernel(
                     "n r c -> r n c"
                 ),
             )
-        load_x(2)
-        for i in range(N_GROUPS):
+        load_x(2, 1)
+        load_pw(0)
+        for i in range(1, N_GROUPS):
             load_pw(i)
-            if i + 3 < N_GROUPS:
-                load_x(i + 3)
+            if i + 2 < N_GROUPS:
+                load_x(i + 2, 1)
 
         xt = {}
         grouped = {}
@@ -117,18 +125,22 @@ def tile_moietransformerblock_pb_t_e_kernel(
         rstd = {}
         centred = {}
         result = {}
+        shifted = {}
+        repeated = {}
         gain_bias = const.tile([P, NQ, 2, D], F32)
 
         def spread(n):
-            repeated = acc_pool.tile([P, 2, D], F32, name="acc")
+            repeated[n] = acc_pool.tile([P, 2, D], F32, name="acc")
             nc.tensor.matmul(
-                out=repeated[:].rearrange("p v d -> p (v d)"),
+                out=repeated[n][:].rearrange("p v d -> p (v d)"),
                 lhsT=ones[:],
                 rhs=vectors[:, n, :, :].rearrange("p v d -> p (v d)"),
                 start=True,
                 stop=True,
             )
-            nc.vector.tensor_copy(out=gain_bias[:, n, :, :], in_=repeated[:])
+
+        def keep_spread(n):
+            nc.vector.tensor_copy(out=gain_bias[:, n, :, :], in_=repeated[n][:])
 
         def transpose(i):
             words = x_sb[i][:].bitcast(F32)
@@ -147,7 +159,8 @@ def tile_moietransformerblock_pb_t_e_kernel(
             if half == 0:
                 grouped[i] = quant.tile([P, GROUP * P * PACK], BF16, name="grouped", align_bytes=64)
             dst = grouped[i][:].bitcast(F32).rearrange("p (a r u) -> p a r u", a=GROUP, u=2)
-            nc.scalar.copy(
+            copy = nc.vector.tensor_copy if (i, half) == (0, 1) else nc.scalar.copy
+            copy(
                 out=dst[:, 2 * half : 2 * half + 2, :, :],
                 in_=xt[i, half][:].rearrange("p a u r -> p a r u"),
             )
@@ -175,7 +188,7 @@ def tile_moietransformerblock_pb_t_e_kernel(
                 )
 
         def scalar_tiles(i):
-            return GROUP - 1 if i % 2 == 0 else GROUP
+            return GROUP - 1
 
         def take_mean(i):
             mean_var[i] = stat.tile([P, GROUP, 2], F32, name="mean_var")
@@ -210,28 +223,29 @@ def tile_moietransformerblock_pb_t_e_kernel(
                     accum_out=mean_var[i][:, a, 1:2],
                 )
 
-        def take_rstd(i):
-            rstd[i] = stat.tile([P, GROUP], F32, name="rstd")
+        def take_rstd(i, of_vector):
             own = scalar_tiles(i)
-            for first, last, scale in ((0, own, 1.0 / D), (own, GROUP, 1.0)):
-                if first < last:
-                    nc.scalar.activation(
-                        out=rstd[i][:, first:last],
-                        in_=mean_var[i][:, first:last, 1],
-                        func=ACT.Abs_reciprocal_sqrt,
-                        scale=scale,
-                        bias=eps[:],
-                    )
+            if not of_vector:
+                rstd[i] = stat.tile([P, GROUP], F32, name="rstd")
+            first, last, scale = (own, GROUP, 1.0) if of_vector else (0, own, 1.0 / D)
+            nc.scalar.activation(
+                out=rstd[i][:, first:last],
+                in_=mean_var[i][:, first:last, 1],
+                func=ACT.Abs_reciprocal_sqrt,
+                scale=scale,
+                bias=eps[:],
+            )
 
         def add_bias(i):
             n, tiles = place(i)
-            result[i] = res_pool.tile([P, GROUP, D], F32, name="result")
-            nc.vector.tensor_tensor(
-                out=result[i][:],
-                in0=pw_sb[i][:],
-                in1=gain_bias[:, n, 1, :].unsqueeze(1).to_broadcast([P, GROUP, D]),
-                op=ALU.add,
-            )
+            shifted[i] = shift_pool.tile([P, GROUP, D], F32, name="shifted")
+            for engine, first, last in ((nc.vector, POOL_TILES, GROUP), (nc.gpsimd, 0, POOL_TILES)):
+                engine.tensor_tensor(
+                    out=shifted[i][:, first:last, :],
+                    in0=pw_sb[i][:, first:last, :],
+                    in1=gain_bias[:, n, 1, :].unsqueeze(1).to_broadcast([P, last - first, D]),
+                    op=ALU.add,
+                )
 
         def centre(i, first, last):
             n, tiles = place(i)
@@ -249,12 +263,13 @@ def tile_moietransformerblock_pb_t_e_kernel(
 
         def finish(i):
             n, tiles = place(i)
+            result[i] = res_pool.tile([P, GROUP, D], F32, name="result")
             for a in range(GROUP):
                 nc.vector.scalar_tensor_tensor(
                     out=result[i][:, a, :],
                     in0=centred[i][:, a, :],
                     scalar=rstd[i][:, a : a + 1],
-                    in1=result[i][:, a, :],
+                    in1=shifted[i][:, a, :],
                     op0=ALU.mult,
                     op1=ALU.add,
                 )
@@ -263,15 +278,20 @@ def tile_moietransformerblock_pb_t_e_kernel(
         def in_range(i):
             return 0 <= i < N_GROUPS
 
+        def groups_to_shift(i):
+            return {2: (0, 1), 3: (2, 3)}.get(i, (i,) if i > 3 else ())
+
         transpose(0)
         for i in range(N_GROUPS + 3):
             if in_range(i - 1):
-                if (i - 1) % GROUPS_PER_BANK == 0:
-                    spread((i - 1) // GROUPS_PER_BANK)
                 quantise(i - 1)
                 multiply(i - 1)
             if in_range(i + 1):
                 transpose(i + 1)
+            if i == 0:
+                spread(0)
+            if in_range(i + 1) and i > 0 and (i + 1) % GROUPS_PER_BANK == 0:
+                spread((i + 1) // GROUPS_PER_BANK)
             if in_range(i - 2):
                 take_mean(i - 2)
             if in_range(i):
@@ -280,15 +300,17 @@ def tile_moietransformerblock_pb_t_e_kernel(
                 take_variance(i - 2)
             if in_range(i):
                 copy_out(i, 1)
+            for j in groups_to_shift(i):
+                if in_range(j):
+                    if j % GROUPS_PER_BANK == 0:
+                        keep_spread(j // GROUPS_PER_BANK)
+                    add_bias(j)
             if in_range(i - 2):
                 vector_stats(i - 2)
                 centre(i - 2, 0, 2)
                 vector_aggregate(i - 2)
-                take_rstd(i - 2)
-                centre(i - 2, 2, 3)
-            if in_range(i - 1):
-                add_bias(i - 1)
-            if in_range(i - 2):
-                centre(i - 2, 3, GROUP)
+                take_rstd(i - 2, False)
+                take_rstd(i - 2, True)
+                centre(i - 2, 2, GROUP)
             if in_range(i - 3):
                 finish(i - 3)

@@ -54,7 +54,8 @@ def tile_moietransformerblock_pb_t_e_kernel(
         stat = ctx.enter_context(tc.tile_pool(name="stat", bufs=6))
         shift_pool = ctx.enter_context(tc.tile_pool(name="shift", bufs=SHIFTED_BUFS))
         xt_pool = ctx.enter_context(tc.psum_pool(name="xt", bufs=4))
-        acc_pool = ctx.enter_context(tc.psum_pool(name="acc", bufs=4))
+        acc_pool = ctx.enter_context(tc.psum_pool(name="acc", bufs=3))
+        sum_pool = ctx.enter_context(tc.psum_pool(name="sum", bufs=1))
         ctx.enter_context(tc.manual_schedule())
 
         eps = const.tile([P, 1], F32)
@@ -69,6 +70,8 @@ def tile_moietransformerblock_pb_t_e_kernel(
         nc.vector.memset(ones[:], 1.0)
         ident = const.tile([P, P], F32)
         make_identity(nc, ident[:])
+        ident_bf16 = const.tile([P, P], BF16)
+        make_identity(nc, ident_bf16[:])
         w_scales = const.tile([P, NQ * D], U8, align_bytes=64)
         w_scales_i32 = w_scales[:].bitcast(I32).rearrange("p (n c) -> p n c", n=NQ)
         nc.vector.memset(w_scales[:].bitcast(I32), 0)
@@ -126,6 +129,7 @@ def tile_moietransformerblock_pb_t_e_kernel(
         centred = {}
         result = {}
         shifted = {}
+        summed = {}
         repeated = {}
         gain_bias = const.tile([P, NQ, 2, D], F32)
 
@@ -236,10 +240,30 @@ def tile_moietransformerblock_pb_t_e_kernel(
                 bias=eps[:],
             )
 
+        def on_tensor(i):
+            return i % 3 != 2
+
+        def add_on_tensor(i):
+            n, tiles = place(i)
+            summed[i] = sum_pool.tile([P, D], F32, name="summed")
+            nc.tensor.matmul(
+                out=summed[i][:], lhsT=ones[:], rhs=vectors[:, n, 1, :], start=True, stop=False
+            )
+            nc.tensor.matmul(
+                out=summed[i][:],
+                lhsT=ident_bf16[:],
+                rhs=pw_sb[i][:, GROUP - 1, :],
+                start=False,
+                stop=True,
+            )
+
         def add_bias(i):
             n, tiles = place(i)
             shifted[i] = shift_pool.tile([P, GROUP, D], F32, name="shifted")
-            for engine, first, last in ((nc.vector, POOL_TILES, GROUP), (nc.gpsimd, 0, POOL_TILES)):
+            shares = [(nc.gpsimd, 0, POOL_TILES)]
+            if not on_tensor(i):
+                shares = [(nc.vector, POOL_TILES, GROUP)] + shares
+            for engine, first, last in shares:
                 engine.tensor_tensor(
                     out=shifted[i][:, first:last, :],
                     in0=pw_sb[i][:, first:last, :],
@@ -269,7 +293,7 @@ def tile_moietransformerblock_pb_t_e_kernel(
                     out=result[i][:, a, :],
                     in0=centred[i][:, a, :],
                     scalar=rstd[i][:, a : a + 1],
-                    in1=shifted[i][:, a, :],
+                    in1=summed[i][:] if a >= POOL_TILES and on_tensor(i) else shifted[i][:, a, :],
                     op0=ALU.mult,
                     op1=ALU.add,
                 )
@@ -283,6 +307,8 @@ def tile_moietransformerblock_pb_t_e_kernel(
 
         transpose(0)
         for i in range(N_GROUPS + 3):
+            if in_range(i - 3) and on_tensor(i - 3):
+                add_on_tensor(i - 3)
             if in_range(i - 1):
                 quantise(i - 1)
                 multiply(i - 1)

@@ -123,7 +123,6 @@ def tile_moietransformerblock_pb_t_e_kernel(
         scales = {}
         acc = {}
         mean_var = {}
-        halves = {}
         scaled_x = {}
         rstd = {}
         centred = {}
@@ -192,10 +191,10 @@ def tile_moietransformerblock_pb_t_e_kernel(
                 )
 
         def scalar_tiles(i):
-            return GROUP - 1
+            return GROUP - 2
 
         def take_mean(i):
-            mean_var[i] = stat.tile([P, GROUP, 2], F32, name="mean_var")
+            mean_var[i] = stat.tile([P, GROUP, 3], F32, name="mean_var")
             scaled_x[i] = work.tile([P, GROUP, D], F32, name="scaled_x")
             for a in range(scalar_tiles(i)):
                 nc.scalar.activation(
@@ -203,17 +202,15 @@ def tile_moietransformerblock_pb_t_e_kernel(
                     in_=acc[i][:, a, :],
                     func=ACT.Copy,
                     scale=1.0 / D,
-                    accum_out=mean_var[i][:, a, 0:1],
+                    accum_out=mean_var[i][:, a, 1:2],
                 )
 
         def vector_stats(i):
-            for a in range(scalar_tiles(i), GROUP):
-                halves[i, a] = stat.tile([P, 6], F32, name="halves")
-                nc.vector.bn_stats(out=halves[i, a][:], in_=acc[i][:, a, :])
-
-        def vector_aggregate(i):
-            for a in range(scalar_tiles(i), GROUP):
-                nc.vector.bn_aggr(out=mean_var[i][:, a, :], in_=halves[i, a][:])
+            first = scalar_tiles(i)
+            nc.vector.bn_stats(
+                out=mean_var[i][:, first:GROUP, :].rearrange("p a s -> p (a s)"),
+                in_=acc[i][:, first:GROUP, :].rearrange("p a d -> p d a"),
+            )
 
         def take_variance(i):
             unused = work.tile([P, GROUP, D], BF16, name="unused")
@@ -223,20 +220,17 @@ def tile_moietransformerblock_pb_t_e_kernel(
                     in_=scaled_x[i][:, a, :],
                     func=ACT.Square,
                     scale=-1.0 * D,
-                    bias=mean_var[i][:, a, 0:1],
-                    accum_out=mean_var[i][:, a, 1:2],
+                    bias=mean_var[i][:, a, 1:2],
+                    accum_out=mean_var[i][:, a, 2:3],
                 )
 
-        def take_rstd(i, of_vector):
-            own = scalar_tiles(i)
-            if not of_vector:
-                rstd[i] = stat.tile([P, GROUP], F32, name="rstd")
-            first, last, scale = (own, GROUP, 1.0) if of_vector else (0, own, 1.0 / D)
+        def take_rstd(i):
+            rstd[i] = stat.tile([P, GROUP], F32, name="rstd")
             nc.scalar.activation(
-                out=rstd[i][:, first:last],
-                in_=mean_var[i][:, first:last, 1],
+                out=rstd[i][:],
+                in_=mean_var[i][:, :, 2],
                 func=ACT.Abs_reciprocal_sqrt,
-                scale=scale,
+                scale=1.0 / D,
                 bias=eps[:],
             )
 
@@ -279,7 +273,7 @@ def tile_moietransformerblock_pb_t_e_kernel(
                 nc.vector.scalar_tensor_tensor(
                     out=centred[i][:, a, :],
                     in0=acc[i][:, a, :],
-                    scalar=mean_var[i][:, a, 0:1],
+                    scalar=mean_var[i][:, a, 1:2],
                     in1=gain_bias[:, n, 0, :],
                     op0=ALU.subtract,
                     op1=ALU.mult,
@@ -333,10 +327,7 @@ def tile_moietransformerblock_pb_t_e_kernel(
                     add_bias(j)
             if in_range(i - 2):
                 vector_stats(i - 2)
-                centre(i - 2, 0, 2)
-                vector_aggregate(i - 2)
-                take_rstd(i - 2, False)
-                take_rstd(i - 2, True)
-                centre(i - 2, 2, GROUP)
+                take_rstd(i - 2)
+                centre(i - 2, 0, GROUP)
             if in_range(i - 3):
                 finish(i - 3)

@@ -26,6 +26,7 @@ GROUP = 4
 GROUPS_PER_BANK = TILES // GROUP
 N_GROUPS = NQ * GROUPS_PER_BANK
 POOL_TILES = 3
+FOLD = 2
 SHIFTED_BUFS = 4
 
 FLOPS = 2 * NQ * F * K * D
@@ -54,7 +55,8 @@ def tile_moietransformerblock_pb_t_e_kernel(
         stat = ctx.enter_context(tc.tile_pool(name="stat", bufs=6))
         shift_pool = ctx.enter_context(tc.tile_pool(name="shift", bufs=SHIFTED_BUFS))
         xt_pool = ctx.enter_context(tc.psum_pool(name="xt", bufs=4))
-        acc_pool = ctx.enter_context(tc.psum_pool(name="acc", bufs=3))
+        acc_pool = ctx.enter_context(tc.psum_pool(name="acc", bufs=2))
+        flip_pool = ctx.enter_context(tc.psum_pool(name="flip", bufs=1))
         sum_pool = ctx.enter_context(tc.psum_pool(name="sum", bufs=1))
         ctx.enter_context(tc.manual_schedule())
 
@@ -129,13 +131,22 @@ def tile_moietransformerblock_pb_t_e_kernel(
         result = {}
         shifted = {}
         summed = {}
+        flip = {}
+        flipped = {}
+        centring = const.tile([P, NQ, D], F32)
+        less_mean = const.tile([P, P], F32)
         repeated = {}
         gain_bias = const.tile([P, NQ, 2, D], F32)
+        bias_cols = const.tile([P, NQ, P], F32)
 
         def spread(n):
-            repeated[n] = acc_pool.tile([P, 2, D], F32, name="acc")
+            if n == 0:
+                repeated["flip"] = flip_pool.tile([P, 2, 2, D], F32, name="flip")
+            if n == NQ - 1:
+                repeated["sum"] = sum_pool.tile([P, 2, D], F32, name="summed")
+            repeated[n] = repeated["sum"][:] if n == NQ - 1 else repeated["flip"][:, n, :, :]
             nc.tensor.matmul(
-                out=repeated[n][:].rearrange("p v d -> p (v d)"),
+                out=repeated[n].rearrange("p v d -> p (v d)"),
                 lhsT=ones[:],
                 rhs=vectors[:, n, :, :].rearrange("p v d -> p (v d)"),
                 start=True,
@@ -143,7 +154,15 @@ def tile_moietransformerblock_pb_t_e_kernel(
             )
 
         def keep_spread(n):
-            nc.vector.tensor_copy(out=gain_bias[:, n, :, :], in_=repeated[n][:])
+            nc.vector.tensor_copy(out=gain_bias[:, n, :, :], in_=repeated[n])
+
+        turned = {}
+
+        def keep_bias():
+            nc.scalar.copy(out=bias_cols[:], in_=turned[0][:])
+
+        def turn_bias(n):
+            nc.tensor.transpose(turned[0][:, n, :], gain_bias[:, n, 1, :], ident[:])
 
         def transpose(i):
             words = x_sb[i][:].bitcast(F32)
@@ -190,8 +209,38 @@ def tile_moietransformerblock_pb_t_e_kernel(
                     stop=True,
                 )
 
+        def folded(i):
+            return 6 <= i < N_GROUPS - 2 and i % 2 == 0
+
+        def make_centring(n):
+            if n == 0:
+                nc.gpsimd.tensor_scalar(
+                    out=less_mean[:], in0=ident[:], scalar1=1.0, scalar2=-1.0 / D, op0=ALU.mult, op1=ALU.add
+                )
+            nc.gpsimd.tensor_tensor(
+                out=centring[:, n, :], in0=less_mean[:], in1=gain_bias[:, n, 0, :], op=ALU.mult
+            )
+
+        def flip_product(i):
+            n, tiles = place(i)
+            rows = slice(FOLD * P, (FOLD + 1) * P)
+            flip[i] = flip_pool.tile([P, P], F32, name="flip")
+            nc.tensor.matmul_mx(
+                out=flip[i][:],
+                lhsT=w_words[:, n * D * PACK : (n + 1) * D * PACK].bitcast(FP8X4),
+                lhsT_scale=w_scales[:, n * D : (n + 1) * D],
+                rhs=codes[i][:, rows].bitcast(FP8X4),
+                rhs_scale=scales[i][:, rows],
+                start=True,
+                stop=True,
+            )
+
+        def keep_flip(i):
+            flipped[i] = work.tile([P, P], F32, name="flipped")
+            nc.scalar.copy(out=flipped[i][:], in_=flip[i][:])
+
         def scalar_tiles(i):
-            return GROUP - 2
+            return GROUP if i >= N_GROUPS - 2 else GROUP - 2
 
         def take_mean(i):
             mean_var[i] = stat.tile([P, GROUP, 3], F32, name="mean_var")
@@ -207,6 +256,8 @@ def tile_moietransformerblock_pb_t_e_kernel(
 
         def vector_stats(i):
             first = scalar_tiles(i)
+            if first == GROUP:
+                return
             nc.vector.bn_stats(
                 out=mean_var[i][:, first:GROUP, :].rearrange("p a s -> p (a s)"),
                 in_=acc[i][:, first:GROUP, :].rearrange("p a d -> p d a"),
@@ -234,42 +285,50 @@ def tile_moietransformerblock_pb_t_e_kernel(
                 bias=eps[:],
             )
 
-        def on_tensor(i):
-            return i % 3 != 2
-
         def add_on_tensor(i):
             n, tiles = place(i)
-            summed[i] = sum_pool.tile([P, D], F32, name="summed")
+            summed[i] = sum_pool.tile([P, 2, D], F32, name="summed")
             nc.tensor.matmul(
-                out=summed[i][:], lhsT=ones[:], rhs=vectors[:, n, 1, :], start=True, stop=False
+                out=summed[i][:, 0, :],
+                lhsT=bias_cols[:, n, :],
+                rhs=ident[:],
+                start=True,
+                stop=False,
+                is_transpose=True,
             )
             nc.tensor.matmul(
-                out=summed[i][:],
+                out=summed[i][:, 0, :],
                 lhsT=ident_bf16[:],
                 rhs=pw_sb[i][:, GROUP - 1, :],
                 start=False,
                 stop=True,
             )
+            if folded(i):
+                nc.tensor.matmul(
+                    out=summed[i][:, 1, :],
+                    lhsT=flipped[i][:],
+                    rhs=centring[:, n, :],
+                    start=True,
+                    stop=True,
+                )
 
         def add_bias(i):
             n, tiles = place(i)
-            shifted[i] = shift_pool.tile([P, GROUP, D], F32, name="shifted")
-            shares = [(nc.gpsimd, 0, POOL_TILES)]
-            if not on_tensor(i):
-                shares = [(nc.vector, POOL_TILES, GROUP)] + shares
-            for engine, first, last in shares:
-                engine.tensor_tensor(
-                    out=shifted[i][:, first:last, :],
-                    in0=pw_sb[i][:, first:last, :],
-                    in1=gain_bias[:, n, 1, :].unsqueeze(1).to_broadcast([P, last - first, D]),
-                    op=ALU.add,
-                )
+            shifted[i] = shift_pool.tile([P, POOL_TILES, D], F32, name="shifted")
+            nc.gpsimd.tensor_tensor(
+                out=shifted[i][:],
+                in0=pw_sb[i][:, 0:POOL_TILES, :],
+                in1=gain_bias[:, n, 1, :].unsqueeze(1).to_broadcast([P, POOL_TILES, D]),
+                op=ALU.add,
+            )
 
         def centre(i, first, last):
             n, tiles = place(i)
             if first == 0:
                 centred[i] = work.tile([P, GROUP, D], F32, name="centred")
             for a in range(first, last):
+                if a == FOLD and folded(i):
+                    continue
                 nc.vector.scalar_tensor_tensor(
                     out=centred[i][:, a, :],
                     in0=acc[i][:, a, :],
@@ -285,13 +344,19 @@ def tile_moietransformerblock_pb_t_e_kernel(
             for a in range(GROUP):
                 nc.vector.scalar_tensor_tensor(
                     out=result[i][:, a, :],
-                    in0=centred[i][:, a, :],
+                    in0=summed[i][:, 1, :] if a == FOLD and folded(i) else centred[i][:, a, :],
                     scalar=rstd[i][:, a : a + 1],
-                    in1=summed[i][:] if a >= POOL_TILES and on_tensor(i) else shifted[i][:, a, :],
+                    in1=summed[i][:, 0, :] if a >= POOL_TILES else shifted[i][:, a, :],
                     op0=ALU.mult,
                     op1=ALU.add,
                 )
-            nc.sync.dma_start(out=out_rows[n, :, tiles, :], in_=result[i][:])
+            pieces = 2 if i == N_GROUPS - 1 else 1
+            step = GROUP // pieces
+            for first in range(0, GROUP, step):
+                nc.sync.dma_start(
+                    out=out_rows[n, :, tiles.start + first : tiles.start + first + step, :],
+                    in_=result[i][:, first : first + step, :],
+                )
 
         def in_range(i):
             return 0 <= i < N_GROUPS
@@ -301,17 +366,30 @@ def tile_moietransformerblock_pb_t_e_kernel(
 
         transpose(0)
         for i in range(N_GROUPS + 3):
-            if in_range(i - 3) and on_tensor(i - 3):
+            if in_range(i - 3):
                 add_on_tensor(i - 3)
             if in_range(i - 1):
                 quantise(i - 1)
                 multiply(i - 1)
+                if folded(i - 1):
+                    flip_product(i - 1)
+            if i == 1:
+                for n in range(NQ):
+                    spread(n)
+            if i == 2:
+                turned[0] = flip_pool.tile([P, NQ, P], F32, name="flip")
+                for n in range(NQ):
+                    turn_bias(n)
             if in_range(i + 1):
                 transpose(i + 1)
-            if i == 0:
-                spread(0)
-            if in_range(i + 1) and i > 0 and (i + 1) % GROUPS_PER_BANK == 0:
-                spread((i + 1) // GROUPS_PER_BANK)
+            if i == 1:
+                for n in range(NQ):
+                    keep_spread(n)
+            for j in groups_to_shift(i):
+                if in_range(j):
+                    add_bias(j)
+            if in_range(i - 2) and folded(i - 2):
+                keep_flip(i - 2)
             if in_range(i - 2):
                 take_mean(i - 2)
             if in_range(i):
@@ -320,11 +398,10 @@ def tile_moietransformerblock_pb_t_e_kernel(
                 take_variance(i - 2)
             if in_range(i):
                 copy_out(i, 1)
-            for j in groups_to_shift(i):
-                if in_range(j):
-                    if j % GROUPS_PER_BANK == 0:
-                        keep_spread(j // GROUPS_PER_BANK)
-                    add_bias(j)
+            if i == 2:
+                keep_bias()
+            if i in (4, 5, 6):
+                make_centring(i - 4)
             if in_range(i - 2):
                 vector_stats(i - 2)
                 take_rstd(i - 2)

@@ -341,7 +341,7 @@ def tile_moietransformerblock_pb_t_e_kernel(
         def finish(i):
             n, tiles = place(i)
             result[i] = res_pool.tile([P, GROUP, D], F32, name="result")
-            for a in range(GROUP):
+            for a in reversed(range(GROUP)):
                 nc.vector.scalar_tensor_tensor(
                     out=result[i][:, a, :],
                     in0=summed[i][:, 1, :] if a == FOLD and folded(i) else centred[i][:, a, :],
@@ -352,7 +352,7 @@ def tile_moietransformerblock_pb_t_e_kernel(
                 )
             pieces = 2 if i == N_GROUPS - 1 else 1
             step = GROUP // pieces
-            for first in range(0, GROUP, step):
+            for first in reversed(range(0, GROUP, step)):
                 nc.sync.dma_start(
                     out=out_rows[n, :, tiles.start + first : tiles.start + first + step, :],
                     in_=result[i][:, first : first + step, :],

@@ -26,7 +26,6 @@ GROUP = 4
 GROUPS_PER_BANK = TILES // GROUP
 N_GROUPS = NQ * GROUPS_PER_BANK
 POOL_TILES = 3
-FOLD = 2
 SHIFTED_BUFS = 4
 
 FLOPS = 2 * NQ * F * K * D
@@ -55,8 +54,7 @@ def tile_moietransformerblock_pb_t_e_kernel(
         stat = ctx.enter_context(tc.tile_pool(name="stat", bufs=6))
         shift_pool = ctx.enter_context(tc.tile_pool(name="shift", bufs=SHIFTED_BUFS))
         xt_pool = ctx.enter_context(tc.psum_pool(name="xt", bufs=4))
-        acc_pool = ctx.enter_context(tc.psum_pool(name="acc", bufs=2))
-        flip_pool = ctx.enter_context(tc.psum_pool(name="flip", bufs=1))
+        acc_pool = ctx.enter_context(tc.psum_pool(name="acc", bufs=3))
         sum_pool = ctx.enter_context(tc.psum_pool(name="sum", bufs=1))
         ctx.enter_context(tc.manual_schedule())
 
@@ -131,22 +129,15 @@ def tile_moietransformerblock_pb_t_e_kernel(
         result = {}
         shifted = {}
         summed = {}
-        flip = {}
-        flipped = {}
-        centring = const.tile([P, NQ, D], F32)
-        less_mean = const.tile([P, P], F32)
         repeated = {}
         gain_bias = const.tile([P, NQ, 2, D], F32)
         bias_cols = const.tile([P, NQ, P], F32)
+        turned = {}
 
         def spread(n):
-            if n == 0:
-                repeated["flip"] = flip_pool.tile([P, 2, 2, D], F32, name="flip")
-            if n == NQ - 1:
-                repeated["sum"] = sum_pool.tile([P, 2, D], F32, name="summed")
-            repeated[n] = repeated["sum"][:] if n == NQ - 1 else repeated["flip"][:, n, :, :]
+            repeated[n] = acc_pool.tile([P, 2, D], F32, name="acc")
             nc.tensor.matmul(
-                out=repeated[n].rearrange("p v d -> p (v d)"),
+                out=repeated[n][:].rearrange("p v d -> p (v d)"),
                 lhsT=ones[:],
                 rhs=vectors[:, n, :, :].rearrange("p v d -> p (v d)"),
                 start=True,
@@ -154,15 +145,7 @@ def tile_moietransformerblock_pb_t_e_kernel(
             )
 
         def keep_spread(n):
-            nc.vector.tensor_copy(out=gain_bias[:, n, :, :], in_=repeated[n])
-
-        turned = {}
-
-        def keep_bias():
-            nc.scalar.copy(out=bias_cols[:], in_=turned[0][:])
-
-        def turn_bias(n):
-            nc.tensor.transpose(turned[0][:, n, :], gain_bias[:, n, 1, :], ident[:])
+            nc.vector.tensor_copy(out=gain_bias[:, n, :, :], in_=repeated[n][:])
 
         def transpose(i):
             words = x_sb[i][:].bitcast(F32)
@@ -208,36 +191,6 @@ def tile_moietransformerblock_pb_t_e_kernel(
                     start=True,
                     stop=True,
                 )
-
-        def folded(i):
-            return 6 <= i < N_GROUPS - 2 and i % 2 == 0
-
-        def make_centring(n):
-            if n == 0:
-                nc.gpsimd.tensor_scalar(
-                    out=less_mean[:], in0=ident[:], scalar1=1.0, scalar2=-1.0 / D, op0=ALU.mult, op1=ALU.add
-                )
-            nc.gpsimd.tensor_tensor(
-                out=centring[:, n, :], in0=less_mean[:], in1=gain_bias[:, n, 0, :], op=ALU.mult
-            )
-
-        def flip_product(i):
-            n, tiles = place(i)
-            rows = slice(FOLD * P, (FOLD + 1) * P)
-            flip[i] = flip_pool.tile([P, P], F32, name="flip")
-            nc.tensor.matmul_mx(
-                out=flip[i][:],
-                lhsT=w_words[:, n * D * PACK : (n + 1) * D * PACK].bitcast(FP8X4),
-                lhsT_scale=w_scales[:, n * D : (n + 1) * D],
-                rhs=codes[i][:, rows].bitcast(FP8X4),
-                rhs_scale=scales[i][:, rows],
-                start=True,
-                stop=True,
-            )
-
-        def keep_flip(i):
-            flipped[i] = work.tile([P, P], F32, name="flipped")
-            nc.scalar.copy(out=flipped[i][:], in_=flip[i][:])
 
         def scalar_tiles(i):
             return GROUP if i >= N_GROUPS - 2 else GROUP - 2
@@ -285,50 +238,60 @@ def tile_moietransformerblock_pb_t_e_kernel(
                 bias=eps[:],
             )
 
+        def on_tensor(i):
+            return True
+
+        def turn_biases():
+            turned[0] = acc_pool.tile([P, NQ, P], F32, name="acc")
+            for n in range(NQ):
+                nc.tensor.transpose(turned[0][:, n, :], gain_bias[:, n, 1, :], ident[:])
+
+        def keep_bias():
+            nc.scalar.copy(out=bias_cols[:], in_=turned[0][:])
+
         def add_on_tensor(i):
             n, tiles = place(i)
-            summed[i] = sum_pool.tile([P, 2, D], F32, name="summed")
+            summed[i] = sum_pool.tile([P, D], F32, name="summed")
+            if i >= 8:
+                nc.tensor.matmul(
+                    out=summed[i][:],
+                    lhsT=bias_cols[:, n, :],
+                    rhs=ident[:],
+                    start=True,
+                    stop=False,
+                    is_transpose=True,
+                )
+            else:
+                nc.tensor.matmul(
+                    out=summed[i][:], lhsT=ones[:], rhs=vectors[:, n, 1, :], start=True, stop=False
+                )
             nc.tensor.matmul(
-                out=summed[i][:, 0, :],
-                lhsT=bias_cols[:, n, :],
-                rhs=ident[:],
-                start=True,
-                stop=False,
-                is_transpose=True,
-            )
-            nc.tensor.matmul(
-                out=summed[i][:, 0, :],
+                out=summed[i][:],
                 lhsT=ident_bf16[:],
                 rhs=pw_sb[i][:, GROUP - 1, :],
                 start=False,
                 stop=True,
             )
-            if folded(i):
-                nc.tensor.matmul(
-                    out=summed[i][:, 1, :],
-                    lhsT=flipped[i][:],
-                    rhs=centring[:, n, :],
-                    start=True,
-                    stop=True,
-                )
 
         def add_bias(i):
             n, tiles = place(i)
-            shifted[i] = shift_pool.tile([P, POOL_TILES, D], F32, name="shifted")
-            nc.gpsimd.tensor_tensor(
-                out=shifted[i][:],
-                in0=pw_sb[i][:, 0:POOL_TILES, :],
-                in1=gain_bias[:, n, 1, :].unsqueeze(1).to_broadcast([P, POOL_TILES, D]),
-                op=ALU.add,
-            )
+            shifted[i] = shift_pool.tile([P, GROUP, D], F32, name="shifted")
+            shares = [(nc.gpsimd, 0, POOL_TILES)]
+            if not on_tensor(i):
+                shares = [(nc.vector, POOL_TILES, GROUP)] + shares
+            for engine, first, last in shares:
+                engine.tensor_tensor(
+                    out=shifted[i][:, first:last, :],
+                    in0=pw_sb[i][:, first:last, :],
+                    in1=gain_bias[:, n, 1, :].unsqueeze(1).to_broadcast([P, last - first, D]),
+                    op=ALU.add,
+                )
 
         def centre(i, first, last):
             n, tiles = place(i)
             if first == 0:
                 centred[i] = work.tile([P, GROUP, D], F32, name="centred")
             for a in range(first, last):
-                if a == FOLD and folded(i):
-                    continue
                 nc.vector.scalar_tensor_tensor(
                     out=centred[i][:, a, :],
                     in0=acc[i][:, a, :],
@@ -344,9 +307,9 @@ def tile_moietransformerblock_pb_t_e_kernel(
             for a in reversed(range(GROUP)):
                 nc.vector.scalar_tensor_tensor(
                     out=result[i][:, a, :],
-                    in0=summed[i][:, 1, :] if a == FOLD and folded(i) else centred[i][:, a, :],
+                    in0=centred[i][:, a, :],
                     scalar=rstd[i][:, a : a + 1],
-                    in1=summed[i][:, 0, :] if a >= POOL_TILES else shifted[i][:, a, :],
+                    in1=summed[i][:] if a >= POOL_TILES and on_tensor(i) else shifted[i][:, a, :],
                     op0=ALU.mult,
                     op1=ALU.add,
                 )
@@ -366,20 +329,16 @@ def tile_moietransformerblock_pb_t_e_kernel(
 
         transpose(0)
         for i in range(N_GROUPS + 3):
-            if in_range(i - 3):
+            if in_range(i - 3) and on_tensor(i - 3):
                 add_on_tensor(i - 3)
             if in_range(i - 1):
                 quantise(i - 1)
                 multiply(i - 1)
-                if folded(i - 1):
-                    flip_product(i - 1)
             if i == 1:
                 for n in range(NQ):
                     spread(n)
-            if i == 2:
-                turned[0] = flip_pool.tile([P, NQ, P], F32, name="flip")
-                for n in range(NQ):
-                    turn_bias(n)
+            if i == 4:
+                turn_biases()
             if in_range(i + 1):
                 transpose(i + 1)
             if i == 1:
@@ -388,8 +347,6 @@ def tile_moietransformerblock_pb_t_e_kernel(
             for j in groups_to_shift(i):
                 if in_range(j):
                     add_bias(j)
-            if in_range(i - 2) and folded(i - 2):
-                keep_flip(i - 2)
             if in_range(i - 2):
                 take_mean(i - 2)
             if in_range(i):
@@ -398,10 +355,8 @@ def tile_moietransformerblock_pb_t_e_kernel(
                 take_variance(i - 2)
             if in_range(i):
                 copy_out(i, 1)
-            if i == 2:
+            if i == 4:
                 keep_bias()
-            if i in (4, 5, 6):
-                make_centring(i - 4)
             if in_range(i - 2):
                 vector_stats(i - 2)
                 take_rstd(i - 2)

@@ -97,7 +97,7 @@ def tile_moietransformerblock_pb_t_e_kernel(
             nc.sync.dma_start(out=pw_sb[i][:], in_=pw_rows[n, :, tiles, :])
 
         load_x(0, 2)
-        load_x(1, 1)
+        load_x(1, 2)
         w_words = const.tile([P, NQ * D * PACK], U8, align_bytes=64)
         nc.sync.dma_start(
             out=w_words[:].bitcast(I32).rearrange("p (n c) -> p n c", n=NQ),
@@ -110,7 +110,7 @@ def tile_moietransformerblock_pb_t_e_kernel(
                     "n r c -> r n c"
                 ),
             )
-        load_x(2, 1)
+        load_x(2, 2)
         load_pw(0)
         for i in range(1, N_GROUPS):
             load_pw(i)
@@ -252,7 +252,7 @@ def tile_moietransformerblock_pb_t_e_kernel(
         def add_on_tensor(i):
             n, tiles = place(i)
             summed[i] = sum_pool.tile([P, D], F32, name="summed")
-            if i >= 8:
+            if i >= 2 and i % 4 != 3:
                 nc.tensor.matmul(
                     out=summed[i][:],
                     lhsT=bias_cols[:, n, :],

from contextlib import ExitStack

import concourse.mybir as mybir
from concourse.masks import make_identity

F32 = mybir.dt.float32
BF16 = mybir.dt.bfloat16
I32 = mybir.dt.int32
U32 = mybir.dt.uint32
U8 = mybir.dt.uint8
FP8X4 = mybir.dt.float8_e4m3fn_x4
ACT = mybir.ActivationFunctionType
ALU = mybir.AluOpType

P = 128
NQ = 3
F = 4096
K = 512
D = 128
LN_EPS = 1e-5

PACK = 4
WORDS = K // 2
TILES = F // P
GROUP = 4
GROUPS_PER_BANK = TILES // GROUP
N_GROUPS = NQ * GROUPS_PER_BANK
POOL_TILES = 3
SHIFTED_BUFS = 4

FLOPS = 2 * NQ * F * K * D


def tile_moietransformerblock_pb_t_e_kernel(
    tc, in_proto, pt_w_words, pt_w_scales, pln_g, pln_b, proto_w, out
):
    nc = tc.nc

    x_rows = in_proto.rearrange("n (p t) k -> n p t k", t=TILES)
    pw_rows = proto_w.rearrange("n (p t) d -> n p t d", t=TILES)
    out_rows = out.rearrange("n (p t) d -> n p t d", t=TILES)

    def place(i):
        n, g = divmod(i, GROUPS_PER_BANK)
        return n, slice(g * GROUP, (g + 1) * GROUP)

    with ExitStack() as ctx:
        const = ctx.enter_context(tc.tile_pool(name="const", bufs=1))
        x_pool = ctx.enter_context(tc.tile_pool(name="x", bufs=N_GROUPS))
        pw_pool = ctx.enter_context(tc.tile_pool(name="pw", bufs=N_GROUPS))
        res_pool = ctx.enter_context(tc.tile_pool(name="res", bufs=N_GROUPS))
        quant = ctx.enter_context(tc.tile_pool(name="quant", bufs=3))
        work = ctx.enter_context(tc.tile_pool(name="work", bufs=3))
        stat = ctx.enter_context(tc.tile_pool(name="stat", bufs=6))
        shift_pool = ctx.enter_context(tc.tile_pool(name="shift", bufs=SHIFTED_BUFS))
        xt_pool = ctx.enter_context(tc.psum_pool(name="xt", bufs=4))
        acc_pool = ctx.enter_context(tc.psum_pool(name="acc", bufs=3))
        sum_pool = ctx.enter_context(tc.psum_pool(name="sum", bufs=1))
        ctx.enter_context(tc.manual_schedule())

        eps = const.tile([P, 1], F32)
        nc.vector.memset(eps[:], LN_EPS)
        table_warmer = const.tile([P, 1], F32)
        nc.scalar.activation(out=table_warmer[:], in_=eps[:], func=ACT.Abs_reciprocal_sqrt)
        vectors = const.tile([P, NQ, 2, D], BF16)
        nc.vector.memset(vectors[:], 0.0)
        for v, vector in enumerate((pln_g, pln_b)):
            nc.scalar.dma_start(out=vectors[0:1, :, v, :], in_=vector.unsqueeze(0))
        ones = const.tile([P, P], BF16)
        nc.vector.memset(ones[:], 1.0)
        ident = const.tile([P, P], F32)
        make_identity(nc, ident[:])
        ident_bf16 = const.tile([P, P], BF16)
        make_identity(nc, ident_bf16[:])
        w_scales = const.tile([P, NQ * D], U8, align_bytes=64)
        w_scales_i32 = w_scales[:].bitcast(I32).rearrange("p (n c) -> p n c", n=NQ)
        nc.vector.memset(w_scales[:].bitcast(I32), 0)

        x_sb = {}
        pw_sb = {}

        def load_x(i, pieces):
            n, tiles = place(i)
            x_sb[i] = x_pool.tile([P, GROUP * K], BF16, name="x_sb")
            step = GROUP // pieces
            for first in range(0, GROUP, step):
                nc.sync.dma_start(
                    out=x_sb[i][:, first * K : (first + step) * K].rearrange(
                        "p (a k) -> p a k", a=step
                    ),
                    in_=x_rows[n, :, tiles.start + first : tiles.start + first + step, :],
                )

        def load_pw(i):
            n, tiles = place(i)
            pw_sb[i] = pw_pool.tile([P, GROUP, D], BF16, name="pw_sb")
            nc.sync.dma_start(out=pw_sb[i][:], in_=pw_rows[n, :, tiles, :])

        load_x(0, 2)
        load_x(1, 2)
        w_words = const.tile([P, NQ * D * PACK], U8, align_bytes=64)
        nc.sync.dma_start(
            out=w_words[:].bitcast(I32).rearrange("p (n c) -> p n c", n=NQ),
            in_=pt_w_words.rearrange("n p d t -> n p (d t)").bitcast(I32).rearrange("n p c -> p n c"),
        )
        for quadrant in range(4):
            nc.sync.dma_start(
                out=w_scales_i32[32 * quadrant : 32 * quadrant + 4, :, :],
                in_=pt_w_scales.bitcast(I32)[:, 4 * quadrant : 4 * quadrant + 4, :].rearrange(
                    "n r c -> r n c"
                ),
            )
        load_x(2, 2)
        load_pw(0)
        for i in range(1, N_GROUPS):
            load_pw(i)
            if i + 2 < N_GROUPS:
                load_x(i + 2, 1)

        xt = {}
        grouped = {}
        codes = {}
        scales = {}
        acc = {}
        mean_var = {}
        scaled_x = {}
        rstd = {}
        centred = {}
        result = {}
        shifted = {}
        summed = {}
        repeated = {}
        gain_bias = const.tile([P, NQ, 2, D], F32)
        bias_cols = const.tile([P, NQ, P], F32)
        turned = {}

        def spread(n):
            repeated[n] = acc_pool.tile([P, 2, D], F32, name="acc")
            nc.tensor.matmul(
                out=repeated[n][:].rearrange("p v d -> p (v d)"),
                lhsT=ones[:],
                rhs=vectors[:, n, :, :].rearrange("p v d -> p (v d)"),
                start=True,
                stop=True,
            )

        def keep_spread(n):
            nc.vector.tensor_copy(out=gain_bias[:, n, :, :], in_=repeated[n][:])

        def transpose(i):
            words = x_sb[i][:].bitcast(F32)
            for half in range(GROUP // 2):
                xt[i, half] = xt_pool.tile([P, 2, 2, P], F32, name="xt")
                for a in range(2):
                    first = (2 * half + a) * WORDS
                    for u in range(2):
                        nc.tensor.transpose(
                            xt[i, half][:, a, u, :],
                            words[:, first + u : first + WORDS : 2],
                            ident[:],
                        )

        def copy_out(i, half):
            if half == 0:
                grouped[i] = quant.tile([P, GROUP * P * PACK], BF16, name="grouped", align_bytes=64)
            dst = grouped[i][:].bitcast(F32).rearrange("p (a r u) -> p a r u", a=GROUP, u=2)
            copy = nc.vector.tensor_copy if (i, half) == (0, 1) else nc.scalar.copy
            copy(
                out=dst[:, 2 * half : 2 * half + 2, :, :],
                in_=xt[i, half][:].rearrange("p a u r -> p a r u"),
            )

        def quantise(i):
            codes[i] = quant.tile([P, GROUP * P], U32, name="codes", align_bytes=64)
            scales[i] = quant.tile([P, GROUP * P], U8, name="scales", align_bytes=64)
            nc.vector.quantize_mx(
                out=codes[i][:].bitcast(FP8X4), scales=scales[i][:], in_=grouped[i][:]
            )

        def multiply(i):
            n, tiles = place(i)
            acc[i] = acc_pool.tile([P, GROUP, D], F32, name="acc")
            for a in range(GROUP):
                rows = slice(a * P, (a + 1) * P)
                nc.tensor.matmul_mx(
                    out=acc[i][:, a, :],
                    lhsT=codes[i][:, rows].bitcast(FP8X4),
                    lhsT_scale=scales[i][:, rows],
                    rhs=w_words[:, n * D * PACK : (n + 1) * D * PACK].bitcast(FP8X4),
                    rhs_scale=w_scales[:, n * D : (n + 1) * D],
                    start=True,
                    stop=True,
                )

        def scalar_tiles(i):
            return GROUP if i >= N_GROUPS - 2 else GROUP - 2

        def take_mean(i):
            mean_var[i] = stat.tile([P, GROUP, 3], F32, name="mean_var")
            scaled_x[i] = work.tile([P, GROUP, D], F32, name="scaled_x")
            for a in range(scalar_tiles(i)):
                nc.scalar.activation(
                    out=scaled_x[i][:, a, :],
                    in_=acc[i][:, a, :],
                    func=ACT.Copy,
                    scale=1.0 / D,
                    accum_out=mean_var[i][:, a, 1:2],
                )

        def vector_stats(i):
            first = scalar_tiles(i)
            if first == GROUP:
                return
            nc.vector.bn_stats(
                out=mean_var[i][:, first:GROUP, :].rearrange("p a s -> p (a s)"),
                in_=acc[i][:, first:GROUP, :].rearrange("p a d -> p d a"),
            )

        def take_variance(i):
            unused = work.tile([P, GROUP, D], BF16, name="unused")
            for a in range(scalar_tiles(i)):
                nc.scalar.activation(
                    out=unused[:, a, :],
                    in_=scaled_x[i][:, a, :],
                    func=ACT.Square,
                    scale=-1.0 * D,
                    bias=mean_var[i][:, a, 1:2],
                    accum_out=mean_var[i][:, a, 2:3],
                )

        def take_rstd(i):
            rstd[i] = stat.tile([P, GROUP], F32, name="rstd")
            nc.scalar.activation(
                out=rstd[i][:],
                in_=mean_var[i][:, :, 2],
                func=ACT.Abs_reciprocal_sqrt,
                scale=1.0 / D,
                bias=eps[:],
            )

        def on_tensor(i):
            return True

        def turn_biases():
            turned[0] = acc_pool.tile([P, NQ, P], F32, name="acc")
            for n in range(NQ):
                nc.tensor.transpose(turned[0][:, n, :], gain_bias[:, n, 1, :], ident[:])

        def keep_bias():
            nc.scalar.copy(out=bias_cols[:], in_=turned[0][:])

        def add_on_tensor(i):
            n, tiles = place(i)
            summed[i] = sum_pool.tile([P, D], F32, name="summed")
            if i >= 2 and i % 4 != 3:
                nc.tensor.matmul(
                    out=summed[i][:],
                    lhsT=bias_cols[:, n, :],
                    rhs=ident[:],
                    start=True,
                    stop=False,
                    is_transpose=True,
                )
            else:
                nc.tensor.matmul(
                    out=summed[i][:], lhsT=ones[:], rhs=vectors[:, n, 1, :], start=True, stop=False
                )
            nc.tensor.matmul(
                out=summed[i][:],
                lhsT=ident_bf16[:],
                rhs=pw_sb[i][:, GROUP - 1, :],
                start=False,
                stop=True,
            )

        def add_bias(i):
            n, tiles = place(i)
            shifted[i] = shift_pool.tile([P, GROUP, D], F32, name="shifted")
            shares = [(nc.gpsimd, 0, POOL_TILES)]
            if not on_tensor(i):
                shares = [(nc.vector, POOL_TILES, GROUP)] + shares
            for engine, first, last in shares:
                engine.tensor_tensor(
                    out=shifted[i][:, first:last, :],
                    in0=pw_sb[i][:, first:last, :],
                    in1=gain_bias[:, n, 1, :].unsqueeze(1).to_broadcast([P, last - first, D]),
                    op=ALU.add,
                )

        def centre(i, first, last):
            n, tiles = place(i)
            if first == 0:
                centred[i] = work.tile([P, GROUP, D], F32, name="centred")
            for a in range(first, last):
                nc.vector.scalar_tensor_tensor(
                    out=centred[i][:, a, :],
                    in0=acc[i][:, a, :],
                    scalar=mean_var[i][:, a, 1:2],
                    in1=gain_bias[:, n, 0, :],
                    op0=ALU.subtract,
                    op1=ALU.mult,
                )

        def finish(i):
            n, tiles = place(i)
            result[i] = res_pool.tile([P, GROUP, D], F32, name="result")
            for a in reversed(range(GROUP)):
                nc.vector.scalar_tensor_tensor(
                    out=result[i][:, a, :],
                    in0=centred[i][:, a, :],
                    scalar=rstd[i][:, a : a + 1],
                    in1=summed[i][:] if a >= POOL_TILES and on_tensor(i) else shifted[i][:, a, :],
                    op0=ALU.mult,
                    op1=ALU.add,
                )
            pieces = 2 if i == N_GROUPS - 1 else 1
            step = GROUP // pieces
            for first in reversed(range(0, GROUP, step)):
                nc.sync.dma_start(
                    out=out_rows[n, :, tiles.start + first : tiles.start + first + step, :],
                    in_=result[i][:, first : first + step, :],
                )

        def in_range(i):
            return 0 <= i < N_GROUPS

        def groups_to_shift(i):
            return {2: (0, 1), 3: (2, 3)}.get(i, (i,) if i > 3 else ())

        transpose(0)
        for i in range(N_GROUPS + 3):
            if in_range(i - 3) and on_tensor(i - 3):
                add_on_tensor(i - 3)
            if in_range(i - 1):
                quantise(i - 1)
                multiply(i - 1)
            if i == 1:
                for n in range(NQ):
                    spread(n)
            if i == 4:
                turn_biases()
            if in_range(i + 1):
                transpose(i + 1)
            if i == 1:
                for n in range(NQ):
                    keep_spread(n)
            for j in groups_to_shift(i):
                if in_range(j):
                    add_bias(j)
            if in_range(i - 2):
                take_mean(i - 2)
            if in_range(i):
                copy_out(i, 0)
            if in_range(i - 2):
                take_variance(i - 2)
            if in_range(i):
                copy_out(i, 1)
            if i == 4:
                keep_bias()
            if in_range(i - 2):
                vector_stats(i - 2)
                take_rstd(i - 2)
                centre(i - 2, 0, GROUP)
            if in_range(i - 3):
                finish(i - 3)
